import numpy as np
import ml_dtypes


def mxq(x, axis, fmt="e4m3"):
    dtype, down = {"e4m3": (ml_dtypes.float8_e4m3fn, 7), "e5m2": (ml_dtypes.float8_e5m2, 14)}[fmt]
    v = np.moveaxis(np.asarray(x, np.float32).astype(ml_dtypes.bfloat16).astype(np.float64), axis, -1)
    blocks = v.reshape(v.shape[:-1] + (-1, 32))
    amax = np.abs(blocks).max(-1, keepdims=True)
    byte = np.maximum(np.where(amax > 0, np.frexp(amax)[1] - 1 + 127, 0) - down, 1)
    scale = np.exp2(byte - 127.0)
    codes = (blocks / scale).astype(np.float32).astype(dtype).astype(np.float64)
    return np.moveaxis((codes * scale).reshape(v.shape), -1, axis)


WIDE = False


def mx_kscale(k):
    if not WIDE:
        return np.ones(k)
    levels = np.array([10, -10, 5, -5, 0])
    a = np.random.permutation(np.resize(levels, k // 512 * 4)).reshape(k // 512, 4)
    idx = np.arange(k)
    return np.exp2(a[idx // 512, idx % 128 // 32])


BF16 = ml_dtypes.bfloat16


def bf(x):
    return np.asarray(x, np.float32).astype(BF16)


def f64(x):
    return np.asarray(x).astype(np.float64)


E2M1 = np.array([0.0, 0.5, 1.0, 1.5, 2.0, 3.0, 4.0, 6.0, -0.0, -0.5, -1.0, -1.5, -2.0, -3.0, -4.0, -6.0])


def pack_weight(w, fmt):
    k, n = w.shape
    w = f64(bf(w)).reshape(k // 32, 32, n)
    amax = np.abs(w).max(1)
    if fmt == "e4m3":
        byte = np.frexp(amax)[1] - 1 + 127 - 7
    else:
        mant, ex = np.frexp(amax / 6.0)
        byte = np.where(mant > 0.5, ex, ex - 1) + 127
    byte = np.clip(np.where(amax > 0, byte, 1), 1, 254)
    scaled = (w * np.exp2(127.0 - byte)[:, None, :]).reshape(k, n).astype(np.float32)
    by_word = np.ascontiguousarray(scaled.reshape(k // 512, 128, 4, n).transpose(0, 1, 3, 2))
    if fmt == "e4m3":
        words = by_word.astype(ml_dtypes.float8_e4m3fn).view(np.uint8)
    else:
        c = by_word.astype(ml_dtypes.float4_e2m1fn).view(np.uint8) & 0xF
        words = c[..., 0::2] | (c[..., 1::2] << 4)
    return np.ascontiguousarray(words), np.ascontiguousarray(byte.astype(np.uint8).reshape(k // 512, 16, n))


def unpack_weight(words, scales, fmt):
    g, p, n, _ = words.shape
    if fmt == "e4m3":
        vals = np.ascontiguousarray(words).view(ml_dtypes.float8_e4m3fn).astype(np.float64)
    else:
        nib = np.empty((g, p, n, 4), np.uint8)
        nib[..., 0::2] = words & 0xF
        nib[..., 1::2] = words >> 4
        vals = E2M1[nib]
    vals = vals * np.repeat(np.exp2(scales.astype(np.float64) - 127.0), 8, axis=1)[..., None]
    return vals.transpose(0, 1, 3, 2).reshape(g * 512, n)

def pack4(w):
    words, scales = pack_weight(w, "e2m1")
    return words.reshape(words.shape[0], 128, -1), scales


def unpack4(words, scales):
    return unpack_weight(words.reshape(words.shape[0], 128, -1, 2), scales, "e2m1")


B, H, W, C, F, K, G, RR = 4, 64, 64, 512, 128, 3, 16, 4
KK = K * K
P = B * H * W


def setup_inputs():
    s = mx_kscale(C)
    x = bf(np.random.standard_normal((B, H, W, C)) * s)
    Wi_words, Wi_scales = pack4(np.random.standard_normal((C, F)) / np.sqrt(C) / s[:, None])
    bi = bf(np.random.standard_normal(F) * 0.3)
    w_span = bf(np.random.standard_normal((B, H, W, KK * G)) * 0.7)
    return {"x": x,
            "Wi_words": Wi_words,
            "Wi_scales": Wi_scales,
            "bi": bi,
            "w_span": w_span}


def reference(x, Wi_words, Wi_scales, bi, w_span):
    xi = ((mxq(f64(x).reshape(P, C), 1, "e4m3") @ unpack4(Wi_words, Wi_scales)) + f64(bi)).reshape(B, H, W, F)
    pad = (K - 1) // 2
    xp = np.pad(xi, ((0, 0), (pad, pad), (pad, pad), (0, 0)))
    patches = np.stack([xp[:, i:i + H, j:j + W, :] for i in range(K) for j in range(K)], axis=-2)
    patches = patches.reshape(B, H, W, G, F // G, KK)
    w = f64(w_span).reshape(B, H, W, G, KK)[:, :, :, :, None, :]
    return (w * patches).sum(-1).reshape(B, H, W, F)

@@ -1,0 +1,254 @@
+from contextlib import ExitStack
+
+import concourse.mybir as mybir
+from concourse.masks import make_identity
+
+F32 = mybir.dt.float32
+BF16 = mybir.dt.bfloat16
+I32 = mybir.dt.int32
+U32 = mybir.dt.uint32
+U8 = mybir.dt.uint8
+FP8X4 = mybir.dt.float8_e4m3fn_x4
+FP4X4 = mybir.dt.float4_e2m1fn_x4
+
+P = 128
+IMAGES, H, W, C, F = 4, 64, 64, 512, 128
+PAIRS = IMAGES // 2
+TAPS = 9
+GROUPS = 16
+PER_GROUP = F // GROUPS
+GROUP_COLS = PER_GROUP * TAPS
+CHUNK = 4
+CHUNKS_PER_PAIR = H // CHUNK
+CHUNKS = PAIRS * CHUNKS_PER_PAIR
+BANK = 512
+PAD = 8
+ROW_COLS = PAD + P + PAD
+LOAD_AHEAD = 4
+TAP_LAG = 3
+
+FLOPS = 2 * IMAGES * H * W * C * F + 2 * IMAGES * H * W * TAPS * F
+
+
+def first_group(i):
+    return -(-3 * P * i // GROUP_COLS)
+
+
+def tile_involution2d_pa_t_kernel(tc, x, Wi_words, Wi_scales, bi, w_span, out):
+    nc = tc.nc
+    mult = mybir.AluOpType.mult
+    identity_fn = mybir.ActivationFunctionType.Identity
+
+    with ExitStack() as ctx:
+        const = ctx.enter_context(tc.tile_pool(name="const", bufs=1))
+        x_pool = ctx.enter_context(tc.tile_pool(name="x_pool", bufs=LOAD_AHEAD))
+        w_pool = ctx.enter_context(tc.tile_pool(name="w_pool", bufs=LOAD_AHEAD + 3))
+        q_pool = ctx.enter_context(tc.tile_pool(name="q_pool", bufs=2))
+        prod_pool = ctx.enter_context(tc.tile_pool(name="prod_pool", bufs=TAP_LAG + 3))
+        out_pool = ctx.enter_context(tc.tile_pool(name="out_pool", bufs=3))
+        ps_x = ctx.enter_context(tc.psum_pool(name="ps_x", bufs=2))
+        ps_xi = ctx.enter_context(tc.psum_pool(name="ps_xi", bufs=1))
+        ps_win = ctx.enter_context(tc.psum_pool(name="ps_win", bufs=3))
+        ps_sum = ctx.enter_context(tc.psum_pool(name="ps_sum", bufs=1))
+        ps_out = ctx.enter_context(tc.psum_pool(name="ps_out", bufs=1))
+        ctx.enter_context(tc.manual_schedule())
+
+        ident = const.tile([P, P], F32)
+        make_identity(nc, ident[:])
+
+        wi_codes = const.tile([P, 2 * F], U8, align_bytes=64)
+        wi_plane = const.tile([P, F], U8, align_bytes=64)
+        nc.vector.memset(wi_plane[:].bitcast(I32), 0)
+        nc.sync.dma_start(out=wi_codes[:].bitcast(I32), in_=Wi_words[0].bitcast(I32))
+        for quadrant in range(4):
+            nc.sync.dma_start(
+                out=wi_plane[32 * quadrant : 32 * quadrant + 4, :].bitcast(I32),
+                in_=Wi_scales[0, 4 * quadrant : 4 * quadrant + 4, :].bitcast(I32),
+            )
+
+        bias_bf = const.tile([P, F], BF16)
+        nc.vector.memset(bias_bf[:], 0.0)
+        nc.sync.dma_start(out=bias_bf[0:1, :], in_=bi.rearrange("(o f) -> o f", o=1))
+        bias_rows = const.tile([P, F], F32)
+        nc.vector.tensor_copy(out=bias_rows[:], in_=bias_bf[:])
+        out_ps = ps_out.tile([P, BANK], F32)
+        nc.tensor.transpose(out_ps[:, 0:P], bias_rows[:], ident[:])
+        bias_col = const.tile([P, 1], F32)
+        nc.vector.tensor_copy(out=bias_col[:], in_=out_ps[:, 0:1])
+
+        xi_img = []
+        for pair in range(PAIRS):
+            xi_pair = const.tile([P, H + 2, ROW_COLS], F32, name="xi_pair%d" % pair)
+            nc.gpsimd.memset(xi_pair[:, :, 0:PAD], 0.0)
+            nc.gpsimd.memset(xi_pair[:, :, PAD + P : ROW_COLS], 0.0)
+            nc.gpsimd.memset(xi_pair[:, 0, PAD : PAD + P], 0.0)
+            nc.gpsimd.memset(xi_pair[:, H + 1, PAD : PAD + P], 0.0)
+            xi_img.append(xi_pair)
+
+        x_of, w_of, grouped_of, codes_of, plane_of = {}, {}, {}, {}, {}
+        prod_of, sum_of, parked_of = {}, {}, {}
+
+        def load_chunk(ch):
+            pair, u0 = ch // CHUNKS_PER_PAIR, CHUNK * (ch % CHUNKS_PER_PAIR)
+            x_rows = x_pool.tile([P, CHUNK, C], BF16)
+            w_rows = w_pool.tile([P, CHUNK, GROUPS * TAPS], BF16)
+            for b2 in range(2):
+                image = 2 * pair + b2
+                nc.sync.dma_start(
+                    out=x_rows[b2:P:2, :, :],
+                    in_=x[image, u0 : u0 + CHUNK].rearrange("u v k -> v u k"),
+                )
+                nc.sync.dma_start(
+                    out=w_rows[b2:P:2, :, :],
+                    in_=w_span[image, u0 : u0 + CHUNK].rearrange("u v r -> v u r"),
+                )
+            x_of[ch], w_of[ch] = x_rows, w_rows
+
+        def turn_chunk(ch):
+            grouped = q_pool.tile([P, CHUNK * P, 4], BF16, align_bytes=64)
+            grouped_words = grouped[:].bitcast(F32)
+            for first in range(0, CHUNK, 2):
+                turned = ps_x.tile([P, 2, 2, P], F32)
+                for s in range(2):
+                    words = x_of[ch][:, first + s, :].bitcast(F32)
+                    for half in range(2):
+                        nc.tensor.transpose(
+                            turned[:, s, half, :], words[:, half : C // 2 : 2], ident[:]
+                        )
+                nc.scalar.copy(
+                    out=grouped_words[:, first * P : (first + 2) * P, :].rearrange(
+                        "p (s n) h -> p s n h", s=2
+                    ),
+                    in_=turned[:].rearrange("p s h n -> p s n h"),
+                )
+            grouped_of[ch] = grouped
+
+        def quantise_chunk(ch):
+            codes = q_pool.tile([P, CHUNK * P], U32, align_bytes=64)
+            plane = q_pool.tile([P, CHUNK * P], U8, align_bytes=64)
+            nc.vector.quantize_mx(
+                out=codes[:].bitcast(FP8X4),
+                scales=plane[:],
+                in_=grouped_of[ch][:].rearrange("p n t -> p (n t)"),
+            )
+            codes_of[ch], plane_of[ch] = codes, plane
+
+        def project_chunk(ch):
+            pair, u0 = ch // CHUNKS_PER_PAIR, CHUNK * (ch % CHUNKS_PER_PAIR)
+            xi_ps = ps_xi.tile([P, BANK], F32)
+            nc.tensor.matmul_mx(
+                out=xi_ps[:],
+                lhsT=wi_codes[:].bitcast(FP4X4),
+                lhsT_scale=wi_plane[:],
+                rhs=codes_of[ch][:].bitcast(FP8X4),
+                rhs_scale=plane_of[ch][:],
+                start=True,
+                stop=True,
+            )
+            nc.scalar.activation(
+                out=xi_img[pair][:, 1 + u0 : 1 + u0 + CHUNK, PAD : PAD + P],
+                in_=xi_ps[:].rearrange("c (u n) -> c u n", u=CHUNK),
+                func=identity_fn,
+                bias=bias_col[:, 0:1],
+                scale=1.0,
+            )
+
+        def cut_windows(pair, r):
+            win = ps_win.tile([P, BANK], F32)
+            for j in range(3):
+                start = PAD - 2 + 2 * j
+                nc.tensor.transpose(
+                    win[:, P * j : P * (j + 1)], xi_img[pair][:, r + 1, start : start + P], ident[:]
+                )
+            if r < H:
+                nc.tensor.transpose(
+                    win[:, 3 * P : 4 * P], xi_img[pair][:, r + 2, PAD - 2 : PAD - 2 + P], ident[:]
+                )
+            return win
+
+        def multiply_windows(pair, r, win):
+            for i in range(3):
+                u = r + 1 - i
+                if 0 <= u < H:
+                    if i == 0:
+                        prod = prod_pool.tile([P, TAPS, F], F32)
+                        prod_of[(pair, u)] = prod
+                    g0, g1 = first_group(i), first_group(i + 1)
+                    col = GROUP_COLS * g0 - 3 * P * i
+                    weights = w_of[pair * CHUNKS_PER_PAIR + u // CHUNK][:, u % CHUNK, TAPS * g0 : TAPS * g1]
+                    nc.vector.tensor_tensor(
+                        out=prod_of[(pair, u)][:, :, PER_GROUP * g0 : PER_GROUP * g1].rearrange(
+                            "p m (g e) -> p m g e", e=PER_GROUP
+                        ),
+                        in0=win[:, col : col + GROUP_COLS * (g1 - g0)].rearrange(
+                            "p (g e m) -> p m g e", e=PER_GROUP, m=TAPS
+                        ),
+                        in1=weights.rearrange("p (g m) -> p m g", m=TAPS)
+                        .unsqueeze(3)
+                        .to_broadcast([P, TAPS, g1 - g0, PER_GROUP]),
+                        op=mult,
+                    )
+
+        def add_taps(pair, u):
+            slot = u % CHUNK
+            if slot == 0:
+                sum_ps = ps_sum.tile([P, BANK], F32)
+                sum_of[pair] = sum_ps
+            for m in range(TAPS):
+                nc.tensor.matmul(
+                    out=sum_of[pair][:, P * slot : P * (slot + 1)],
+                    lhsT=prod_of[(pair, u)][:, m, :],
+                    rhs=ident[:],
+                    is_transpose=True,
+                    start=(m == 0),
+                    stop=(m == TAPS - 1),
+                )
+
+        def park_sums(pair):
+            sum_sb = out_pool.tile([P, BANK], F32)
+            nc.scalar.copy(out=sum_sb[:], in_=sum_of[pair][:])
+            parked_of[pair] = sum_sb
+
+        def store_rows(pair, u0):
+            back_ps = ps_out.tile([P, BANK], F32, tag="out_ps")
+            for slot in range(CHUNK):
+                cols = slice(P * slot, P * (slot + 1))
+                nc.tensor.transpose(back_ps[:, cols], parked_of[pair][:, cols], ident[:])
+            out_rows = out_pool.tile([P, CHUNK, F], F32)
+            nc.scalar.copy(out=out_rows[:], in_=back_ps[:].rearrange("p (u o) -> p u o", u=CHUNK))
+            for b2 in range(2):
+                nc.scalar.dma_start(
+                    out=out[2 * pair + b2, u0 : u0 + CHUNK].rearrange("u v o -> v u o"),
+                    in_=out_rows[b2:P:2, :, :],
+                )
+
+        for ch in range(LOAD_AHEAD):
+            load_chunk(ch)
+        turn_chunk(0)
+        quantise_chunk(0)
+        project_chunk(0)
+        turn_chunk(1)
+        quantise_chunk(1)
+
+        for pair in range(PAIRS):
+            for r in range(-1, H + TAP_LAG + 2):
+                ch = pair * CHUNKS_PER_PAIR + (r + 1) // CHUNK
+                in_image = r < H - 1
+                if in_image and r % CHUNK == 3:
+                    if ch + LOAD_AHEAD < CHUNKS:
+                        load_chunk(ch + LOAD_AHEAD)
+                    if ch + 1 < CHUNKS:
+                        project_chunk(ch + 1)
+                    if ch + 2 < CHUNKS:
+                        turn_chunk(ch + 2)
+                if r <= H:
+                    multiply_windows(pair, r, cut_windows(pair, r))
+                if in_image and r % CHUNK == 1 and ch + 2 < CHUNKS:
+                    quantise_chunk(ch + 2)
+                if r % CHUNK == 0 and r >= CHUNK + TAP_LAG + 1:
+                    store_rows(pair, r - CHUNK - TAP_LAG - 1)
+                u = r - TAP_LAG
+                if 0 <= u < H:
+                    add_taps(pair, u)
+                    if u % CHUNK == CHUNK - 1:
+                        park_sums(pair)

@@ -43,6 +43,7 @@ def tile_involution2d_pa_t_kernel(tc, x, Wi_words, Wi_scales, bi, w_span, out):
         const = ctx.enter_context(tc.tile_pool(name="const", bufs=1))
         x_pool = ctx.enter_context(tc.tile_pool(name="x_pool", bufs=LOAD_AHEAD))
         w_pool = ctx.enter_context(tc.tile_pool(name="w_pool", bufs=LOAD_AHEAD + 3))
+        sort_pool = ctx.enter_context(tc.tile_pool(name="sort_pool", bufs=2))
         q_pool = ctx.enter_context(tc.tile_pool(name="q_pool", bufs=2))
         prod_pool = ctx.enter_context(tc.tile_pool(name="prod_pool", bufs=TAP_LAG + 3))
         out_pool = ctx.enter_context(tc.tile_pool(name="out_pool", bufs=3))
@@ -85,7 +86,7 @@ def tile_involution2d_pa_t_kernel(tc, x, Wi_words, Wi_scales, bi, w_span, out):
             nc.gpsimd.memset(xi_pair[:, H + 1, PAD : PAD + P], 0.0)
             xi_img.append(xi_pair)
 
-        x_of, w_of, grouped_of, codes_of, plane_of = {}, {}, {}, {}, {}
+        x_of, w_of, sorted_of, grouped_of, codes_of, plane_of = {}, {}, {}, {}, {}, {}
         prod_of, sum_of, parked_of = {}, {}, {}
 
         def load_chunk(ch):
@@ -104,16 +105,26 @@ def tile_involution2d_pa_t_kernel(tc, x, Wi_words, Wi_scales, bi, w_span, out):
                 )
             x_of[ch], w_of[ch] = x_rows, w_rows
 
+        def sort_chunk(ch):
+            x_sorted = sort_pool.tile([P, CHUNK, 2, P], F32)
+            nc.scalar.copy(
+                out=x_sorted[:],
+                in_=x_of[ch][:]
+                .rearrange("p s k -> p (s k)")
+                .bitcast(F32)
+                .rearrange("p (s w h) -> p s h w", s=CHUNK, h=2),
+            )
+            sorted_of[ch] = x_sorted
+
         def turn_chunk(ch):
             grouped = q_pool.tile([P, CHUNK * P, 4], BF16, align_bytes=64)
             grouped_words = grouped[:].bitcast(F32)
             for first in range(0, CHUNK, 2):
                 turned = ps_x.tile([P, 2, 2, P], F32)
                 for s in range(2):
-                    words = x_of[ch][:, first + s, :].bitcast(F32)
                     for half in range(2):
                         nc.tensor.transpose(
-                            turned[:, s, half, :], words[:, half : C // 2 : 2], ident[:]
+                            turned[:, s, half, :], sorted_of[ch][:, first + s, half, :], ident[:]
                         )
                 nc.scalar.copy(
                     out=grouped_words[:, first * P : (first + 2) * P, :].rearrange(
@@ -224,14 +235,27 @@ def tile_involution2d_pa_t_kernel(tc, x, Wi_words, Wi_scales, bi, w_span, out):
 
         for ch in range(LOAD_AHEAD):
             load_chunk(ch)
+        sort_chunk(0)
         turn_chunk(0)
+        sort_chunk(1)
         quantise_chunk(0)
         project_chunk(0)
         turn_chunk(1)
+        sort_chunk(2)
         quantise_chunk(1)
 
+        window_steps = [(pair, r) for pair in range(PAIRS) for r in range(-1, H + 1)]
+        step_of = dict((pair_r, step) for step, pair_r in enumerate(window_steps))
+        add_at, store_at = {}, {}
         for pair in range(PAIRS):
-            for r in range(-1, H + TAP_LAG + 2):
+            for u in range(H):
+                add_at[step_of[(pair, u)] + TAP_LAG] = (pair, u)
+            for u0 in range(0, H, CHUNK):
+                store_at[step_of[(pair, u0)] + CHUNK + TAP_LAG + 1] = (pair, u0)
+
+        for step in range(len(window_steps) + TAP_LAG + 2):
+            if step < len(window_steps):
+                pair, r = window_steps[step]
                 ch = pair * CHUNKS_PER_PAIR + (r + 1) // CHUNK
                 in_image = r < H - 1
                 if in_image and r % CHUNK == 3:
@@ -241,14 +265,15 @@ def tile_involution2d_pa_t_kernel(tc, x, Wi_words, Wi_scales, bi, w_span, out):
                         project_chunk(ch + 1)
                     if ch + 2 < CHUNKS:
                         turn_chunk(ch + 2)
-                if r <= H:
-                    multiply_windows(pair, r, cut_windows(pair, r))
+                multiply_windows(pair, r, cut_windows(pair, r))
                 if in_image and r % CHUNK == 1 and ch + 2 < CHUNKS:
                     quantise_chunk(ch + 2)
-                if r % CHUNK == 0 and r >= CHUNK + TAP_LAG + 1:
-                    store_rows(pair, r - CHUNK - TAP_LAG - 1)
-                u = r - TAP_LAG
-                if 0 <= u < H:
-                    add_taps(pair, u)
-                    if u % CHUNK == CHUNK - 1:
-                        park_sums(pair)
+                if in_image and r % CHUNK == 1 and ch + 3 < CHUNKS:
+                    sort_chunk(ch + 3)
+            if step in store_at:
+                store_rows(store_at[step][0], store_at[step][1])
+            if step in add_at:
+                add_pair, u = add_at[step]
+                add_taps(add_pair, u)
+                if u % CHUNK == CHUNK - 1:
+                    park_sums(add_pair)

@@ -24,8 +24,15 @@ CHUNKS = PAIRS * CHUNKS_PER_PAIR
 BANK = 512
 PAD = 8
 ROW_COLS = PAD + P + PAD
-LOAD_AHEAD = 4
-TAP_LAG = 3
+STEPS_PER_PAIR = H + 2
+
+WIN_BANKS = 4
+ADD_LAG = 4
+LOAD_LEAD = 24
+SORT_LEAD = 14
+TURN_LEAD = 10
+STRIDE = 2
+QUANT_LEAD = 5
 
 FLOPS = 2 * IMAGES * H * W * C * F + 2 * IMAGES * H * W * TAPS * F
 
@@ -41,17 +48,16 @@ def tile_involution2d_pa_t_kernel(tc, x, Wi_words, Wi_scales, bi, w_span, out):
 
     with ExitStack() as ctx:
         const = ctx.enter_context(tc.tile_pool(name="const", bufs=1))
-        x_pool = ctx.enter_context(tc.tile_pool(name="x_pool", bufs=LOAD_AHEAD))
-        w_pool = ctx.enter_context(tc.tile_pool(name="w_pool", bufs=LOAD_AHEAD + 3))
-        sort_pool = ctx.enter_context(tc.tile_pool(name="sort_pool", bufs=2))
-        q_pool = ctx.enter_context(tc.tile_pool(name="q_pool", bufs=2))
-        prod_pool = ctx.enter_context(tc.tile_pool(name="prod_pool", bufs=TAP_LAG + 3))
+        x_pool = ctx.enter_context(tc.tile_pool(name="x_pool", bufs=4))
+        w_pool = ctx.enter_context(tc.tile_pool(name="w_pool", bufs=(LOAD_LEAD + 9) // CHUNK + 2))
+        sort_pool = ctx.enter_context(tc.tile_pool(name="sort_pool", bufs=8))
+        q_pool = ctx.enter_context(tc.tile_pool(name="q_pool", bufs=3))
+        prod_pool = ctx.enter_context(tc.tile_pool(name="prod_pool", bufs=ADD_LAG + 4))
         out_pool = ctx.enter_context(tc.tile_pool(name="out_pool", bufs=3))
-        ps_x = ctx.enter_context(tc.psum_pool(name="ps_x", bufs=2))
-        ps_xi = ctx.enter_context(tc.psum_pool(name="ps_xi", bufs=1))
-        ps_win = ctx.enter_context(tc.psum_pool(name="ps_win", bufs=3))
-        ps_sum = ctx.enter_context(tc.psum_pool(name="ps_sum", bufs=1))
-        ps_out = ctx.enter_context(tc.psum_pool(name="ps_out", bufs=1))
+        ps_x = ctx.enter_context(tc.psum_pool(name="ps_x", bufs=1))
+        ps_win = ctx.enter_context(tc.psum_pool(name="ps_win", bufs=WIN_BANKS))
+        ps_sum = ctx.enter_context(tc.psum_pool(name="ps_sum", bufs=2))
+        ps_turns = ctx.enter_context(tc.psum_pool(name="ps_turns", bufs=1))
         ctx.enter_context(tc.manual_schedule())
 
         ident = const.tile([P, P], F32)
@@ -72,10 +78,10 @@ def tile_involution2d_pa_t_kernel(tc, x, Wi_words, Wi_scales, bi, w_span, out):
         nc.sync.dma_start(out=bias_bf[0:1, :], in_=bi.rearrange("(o f) -> o f", o=1))
         bias_rows = const.tile([P, F], F32)
         nc.vector.tensor_copy(out=bias_rows[:], in_=bias_bf[:])
-        out_ps = ps_out.tile([P, BANK], F32)
-        nc.tensor.transpose(out_ps[:, 0:P], bias_rows[:], ident[:])
+        bias_ps = ps_turns.tile([P, BANK], F32, tag="by_turns")
+        nc.tensor.transpose(bias_ps[:, 0:P], bias_rows[:], ident[:])
         bias_col = const.tile([P, 1], F32)
-        nc.vector.tensor_copy(out=bias_col[:], in_=out_ps[:, 0:1])
+        nc.vector.tensor_copy(out=bias_col[:], in_=bias_ps[:, 0:1])
 
         xi_img = []
         for pair in range(PAIRS):
@@ -86,53 +92,50 @@ def tile_involution2d_pa_t_kernel(tc, x, Wi_words, Wi_scales, bi, w_span, out):
             nc.gpsimd.memset(xi_pair[:, H + 1, PAD : PAD + P], 0.0)
             xi_img.append(xi_pair)
 
-        x_of, w_of, sorted_of, grouped_of, codes_of, plane_of = {}, {}, {}, {}, {}, {}
-        prod_of, sum_of, parked_of = {}, {}, {}
+        x_of, w_of, sorted_of, turned_of, grouped_of, codes_of, plane_of = {}, {}, {}, {}, {}, {}, {}
+        win_of, prod_of, sum_of, parked_of = {}, {}, {}, {}
 
         def load_chunk(ch):
             pair, u0 = ch // CHUNKS_PER_PAIR, CHUNK * (ch % CHUNKS_PER_PAIR)
             x_rows = x_pool.tile([P, CHUNK, C], BF16)
             w_rows = w_pool.tile([P, CHUNK, GROUPS * TAPS], BF16)
             for b2 in range(2):
-                image = 2 * pair + b2
                 nc.sync.dma_start(
                     out=x_rows[b2:P:2, :, :],
-                    in_=x[image, u0 : u0 + CHUNK].rearrange("u v k -> v u k"),
+                    in_=x[2 * pair + b2, u0 : u0 + CHUNK].rearrange("u v k -> v u k"),
                 )
+            for b2 in range(2):
                 nc.sync.dma_start(
                     out=w_rows[b2:P:2, :, :],
-                    in_=w_span[image, u0 : u0 + CHUNK].rearrange("u v r -> v u r"),
+                    in_=w_span[2 * pair + b2, u0 : u0 + CHUNK].rearrange("u v r -> v u r"),
                 )
             x_of[ch], w_of[ch] = x_rows, w_rows
 
-        def sort_chunk(ch):
-            x_sorted = sort_pool.tile([P, CHUNK, 2, P], F32)
+        def sort_row(ch, k):
+            x_sorted = sort_pool.tile([P, 2, P], F32)
             nc.scalar.copy(
                 out=x_sorted[:],
-                in_=x_of[ch][:]
-                .rearrange("p s k -> p (s k)")
-                .bitcast(F32)
-                .rearrange("p (s w h) -> p s h w", s=CHUNK, h=2),
+                in_=x_of[ch][:, k, :].bitcast(F32).rearrange("p (w h) -> p h w", h=2),
             )
-            sorted_of[ch] = x_sorted
+            sorted_of[(ch, k)] = x_sorted
 
-        def turn_chunk(ch):
-            grouped = q_pool.tile([P, CHUNK * P, 4], BF16, align_bytes=64)
-            grouped_words = grouped[:].bitcast(F32)
-            for first in range(0, CHUNK, 2):
+        def turn_row(ch, k):
+            if k == 0:
+                grouped = q_pool.tile([P, CHUNK * P, 4], BF16, align_bytes=64)
+                grouped_of[ch] = grouped
+            s = k % 2
+            if s == 0:
                 turned = ps_x.tile([P, 2, 2, P], F32)
-                for s in range(2):
-                    for half in range(2):
-                        nc.tensor.transpose(
-                            turned[:, s, half, :], sorted_of[ch][:, first + s, half, :], ident[:]
-                        )
+                turned_of[ch] = turned
+            for half in range(2):
+                nc.tensor.transpose(turned_of[ch][:, s, half, :], sorted_of[(ch, k)][:, half, :], ident[:])
+            if s == 1:
                 nc.scalar.copy(
-                    out=grouped_words[:, first * P : (first + 2) * P, :].rearrange(
-                        "p (s n) h -> p s n h", s=2
-                    ),
-                    in_=turned[:].rearrange("p s h n -> p s n h"),
+                    out=grouped_of[ch][:]
+                    .bitcast(F32)[:, (k - 1) * P : (k + 1) * P, :]
+                    .rearrange("p (s n) h -> p s n h", s=2),
+                    in_=turned_of[ch][:].rearrange("p s h n -> p s n h"),
                 )
-            grouped_of[ch] = grouped
 
         def quantise_chunk(ch):
             codes = q_pool.tile([P, CHUNK * P], U32, align_bytes=64)
@@ -146,7 +149,7 @@ def tile_involution2d_pa_t_kernel(tc, x, Wi_words, Wi_scales, bi, w_span, out):
 
         def project_chunk(ch):
             pair, u0 = ch // CHUNKS_PER_PAIR, CHUNK * (ch % CHUNKS_PER_PAIR)
-            xi_ps = ps_xi.tile([P, BANK], F32)
+            xi_ps = ps_turns.tile([P, BANK], F32, tag="by_turns")
             nc.tensor.matmul_mx(
                 out=xi_ps[:],
                 lhsT=wi_codes[:].bitcast(FP4X4),
@@ -175,9 +178,10 @@ def tile_involution2d_pa_t_kernel(tc, x, Wi_words, Wi_scales, bi, w_span, out):
                 nc.tensor.transpose(
                     win[:, 3 * P : 4 * P], xi_img[pair][:, r + 2, PAD - 2 : PAD - 2 + P], ident[:]
                 )
-            return win
+            win_of[(pair, r)] = win
 
-        def multiply_windows(pair, r, win):
+        def multiply_windows(pair, r):
+            win = win_of[(pair, r)]
             for i in range(3):
                 u = r + 1 - i
                 if 0 <= u < H:
@@ -214,17 +218,16 @@ def tile_involution2d_pa_t_kernel(tc, x, Wi_words, Wi_scales, bi, w_span, out):
                     start=(m == 0),
                     stop=(m == TAPS - 1),
                 )
+            if slot == CHUNK - 1:
+                sum_sb = out_pool.tile([P, BANK], F32)
+                nc.scalar.copy(out=sum_sb[:], in_=sum_of[pair][:])
+                parked_of[(pair, u - slot)] = sum_sb
 
-        def park_sums(pair):
-            sum_sb = out_pool.tile([P, BANK], F32)
-            nc.scalar.copy(out=sum_sb[:], in_=sum_of[pair][:])
-            parked_of[pair] = sum_sb
-
-        def store_rows(pair, u0):
-            back_ps = ps_out.tile([P, BANK], F32, tag="out_ps")
+        def turn_back(pair, u0):
+            back_ps = ps_turns.tile([P, BANK], F32, tag="by_turns")
             for slot in range(CHUNK):
                 cols = slice(P * slot, P * (slot + 1))
-                nc.tensor.transpose(back_ps[:, cols], parked_of[pair][:, cols], ident[:])
+                nc.tensor.transpose(back_ps[:, cols], parked_of[(pair, u0)][:, cols], ident[:])
             out_rows = out_pool.tile([P, CHUNK, F], F32)
             nc.scalar.copy(out=out_rows[:], in_=back_ps[:].rearrange("p (u o) -> p u o", u=CHUNK))
             for b2 in range(2):
@@ -233,47 +236,30 @@ def tile_involution2d_pa_t_kernel(tc, x, Wi_words, Wi_scales, bi, w_span, out):
                     in_=out_rows[b2:P:2, :, :],
                 )
 
-        for ch in range(LOAD_AHEAD):
-            load_chunk(ch)
-        sort_chunk(0)
-        turn_chunk(0)
-        sort_chunk(1)
-        quantise_chunk(0)
-        project_chunk(0)
-        turn_chunk(1)
-        sort_chunk(2)
-        quantise_chunk(1)
+        plan = {}
 
-        window_steps = [(pair, r) for pair in range(PAIRS) for r in range(-1, H + 1)]
-        step_of = dict((pair_r, step) for step, pair_r in enumerate(window_steps))
-        add_at, store_at = {}, {}
+        def at(step, order, job, *args):
+            plan.setdefault(step // STRIDE, []).append((order, job, args))
+
         for pair in range(PAIRS):
+            first = STEPS_PER_PAIR * pair
+            for r in range(-1, H + 1):
+                at(first + r + 1, 2, cut_windows, pair, r)
+                at(first + r + 1, 3, multiply_windows, pair, r)
             for u in range(H):
-                add_at[step_of[(pair, u)] + TAP_LAG] = (pair, u)
+                at(first + u + 2 + ADD_LAG, 4, add_taps, pair, u)
             for u0 in range(0, H, CHUNK):
-                store_at[step_of[(pair, u0)] + CHUNK + TAP_LAG + 1] = (pair, u0)
+                parked = first + u0 + CHUNK + 1 + ADD_LAG
+                at(parked + 1, 5, turn_back, pair, u0)
+                ch = pair * CHUNKS_PER_PAIR + u0 // CHUNK
+                projected = first + u0 - CHUNK
+                at(projected - LOAD_LEAD, 0, load_chunk, ch)
+                for k in range(CHUNK):
+                    at(projected - SORT_LEAD + k, 1, sort_row, ch, k)
+                    at(projected - TURN_LEAD + k, 6, turn_row, ch, k)
+                at(projected - QUANT_LEAD, 7, quantise_chunk, ch)
+                at(projected, 8, project_chunk, ch)
 
-        for step in range(len(window_steps) + TAP_LAG + 2):
-            if step < len(window_steps):
-                pair, r = window_steps[step]
-                ch = pair * CHUNKS_PER_PAIR + (r + 1) // CHUNK
-                in_image = r < H - 1
-                if in_image and r % CHUNK == 3:
-                    if ch + LOAD_AHEAD < CHUNKS:
-                        load_chunk(ch + LOAD_AHEAD)
-                    if ch + 1 < CHUNKS:
-                        project_chunk(ch + 1)
-                    if ch + 2 < CHUNKS:
-                        turn_chunk(ch + 2)
-                multiply_windows(pair, r, cut_windows(pair, r))
-                if in_image and r % CHUNK == 1 and ch + 2 < CHUNKS:
-                    quantise_chunk(ch + 2)
-                if in_image and r % CHUNK == 1 and ch + 3 < CHUNKS:
-                    sort_chunk(ch + 3)
-            if step in store_at:
-                store_rows(store_at[step][0], store_at[step][1])
-            if step in add_at:
-                add_pair, u = add_at[step]
-                add_taps(add_pair, u)
-                if u % CHUNK == CHUNK - 1:
-                    park_sums(add_pair)
+        for step in sorted(plan):
+            for order, job, args in sorted(plan[step], key=lambda entry: entry[0]):
+                job(*args)

@@ -19,20 +19,25 @@ GROUPS = 16
 PER_GROUP = F // GROUPS
 GROUP_COLS = PER_GROUP * TAPS
 CHUNK = 4
-CHUNKS_PER_PAIR = H // CHUNK
-CHUNKS = PAIRS * CHUNKS_PER_PAIR
+ROWS = PAIRS * H
 BANK = 512
 PAD = 8
 ROW_COLS = PAD + P + PAD
-STEPS_PER_PAIR = H + 2
 
 WIN_BANKS = 4
-ADD_LAG = 4
-LOAD_LEAD = 24
-SORT_LEAD = 14
-TURN_LEAD = 10
-STRIDE = 2
+TAP_BEATS = 2
+BEAT = 2
+
+FIRST_CHUNKS = [(0, 2), (2, 2)]
+CHUNK_ROWS = FIRST_CHUNKS + [(row, CHUNK) for row in range(4, ROWS, CHUNK)]
+
+LEAD = 6
+RATE = 2
+EARLY_ROWS = 12
+VECTOR_SORTS = 4
+SORT_AHEAD = 1
 QUANT_LEAD = 5
+PROJECT_LEAD = 3
 
 FLOPS = 2 * IMAGES * H * W * C * F + 2 * IMAGES * H * W * TAPS * F
 
@@ -48,17 +53,38 @@ def tile_involution2d_pa_t_kernel(tc, x, Wi_words, Wi_scales, bi, w_span, out):
 
     with ExitStack() as ctx:
         const = ctx.enter_context(tc.tile_pool(name="const", bufs=1))
-        x_pool = ctx.enter_context(tc.tile_pool(name="x_pool", bufs=4))
-        w_pool = ctx.enter_context(tc.tile_pool(name="w_pool", bufs=(LOAD_LEAD + 9) // CHUNK + 2))
-        sort_pool = ctx.enter_context(tc.tile_pool(name="sort_pool", bufs=8))
+        x_pool = ctx.enter_context(tc.tile_pool(name="x_pool", bufs=6))
+        w_pool = ctx.enter_context(tc.tile_pool(name="w_pool", bufs=5))
+        sort_pool = ctx.enter_context(tc.tile_pool(name="sort_pool", bufs=12))
+        grouped_pool = ctx.enter_context(tc.tile_pool(name="grouped_pool", bufs=7))
         q_pool = ctx.enter_context(tc.tile_pool(name="q_pool", bufs=3))
-        prod_pool = ctx.enter_context(tc.tile_pool(name="prod_pool", bufs=ADD_LAG + 4))
+        prod_pool = ctx.enter_context(tc.tile_pool(name="prod_pool", bufs=2 * TAP_BEATS + 4))
         out_pool = ctx.enter_context(tc.tile_pool(name="out_pool", bufs=3))
         ps_x = ctx.enter_context(tc.psum_pool(name="ps_x", bufs=1))
         ps_win = ctx.enter_context(tc.psum_pool(name="ps_win", bufs=WIN_BANKS))
         ps_sum = ctx.enter_context(tc.psum_pool(name="ps_sum", bufs=2))
         ps_turns = ctx.enter_context(tc.psum_pool(name="ps_turns", bufs=1))
         ctx.enter_context(tc.manual_schedule())
+
+        warm = const.tile([P, 1], F32)
+        nc.vector.memset(warm[:], 0.0)
+        nc.scalar.activation(out=warm[:], in_=warm[:], func=identity_fn, bias=0.0, scale=1.0)
+
+        x_of, w_of, sorted_of, turned_of, grouped_of, codes_of, plane_of = {}, {}, {}, {}, {}, {}, {}
+
+        def load_x(ch):
+            row, count = CHUNK_ROWS[ch]
+            pair, u0 = row // H, row % H
+            x_rows = x_pool.tile([P, CHUNK, C], BF16)
+            for b2 in range(2):
+                nc.sync.dma_start(
+                    out=x_rows[b2:P:2, 0:count, :],
+                    in_=x[2 * pair + b2, u0 : u0 + count].rearrange("u v k -> v u k"),
+                )
+            x_of[ch] = x_rows
+
+        for ch in range(len(FIRST_CHUNKS)):
+            load_x(ch)
 
         ident = const.tile([P, P], F32)
         make_identity(nc, ident[:])
@@ -75,13 +101,17 @@ def tile_involution2d_pa_t_kernel(tc, x, Wi_words, Wi_scales, bi, w_span, out):
 
         bias_bf = const.tile([P, F], BF16)
         nc.vector.memset(bias_bf[:], 0.0)
-        nc.sync.dma_start(out=bias_bf[0:1, :], in_=bi.rearrange("(o f) -> o f", o=1))
+        nc.scalar.dma_start(out=bias_bf[0:1, :], in_=bi.rearrange("(o f) -> o f", o=1))
         bias_rows = const.tile([P, F], F32)
-        nc.vector.tensor_copy(out=bias_rows[:], in_=bias_bf[:])
-        bias_ps = ps_turns.tile([P, BANK], F32, tag="by_turns")
-        nc.tensor.transpose(bias_ps[:, 0:P], bias_rows[:], ident[:])
         bias_col = const.tile([P, 1], F32)
-        nc.vector.tensor_copy(out=bias_col[:], in_=bias_ps[:, 0:1])
+
+        def widen_bias():
+            nc.vector.tensor_copy(out=bias_rows[:], in_=bias_bf[:])
+
+        def turn_bias():
+            bias_ps = ps_turns.tile([P, BANK], F32, tag="by_turns")
+            nc.tensor.transpose(bias_ps[:, 0:P], bias_rows[:], ident[:])
+            nc.vector.tensor_copy(out=bias_col[:], in_=bias_ps[:, 0:1])
 
         xi_img = []
         for pair in range(PAIRS):
@@ -92,41 +122,39 @@ def tile_involution2d_pa_t_kernel(tc, x, Wi_words, Wi_scales, bi, w_span, out):
             nc.gpsimd.memset(xi_pair[:, H + 1, PAD : PAD + P], 0.0)
             xi_img.append(xi_pair)
 
-        x_of, w_of, sorted_of, turned_of, grouped_of, codes_of, plane_of = {}, {}, {}, {}, {}, {}, {}
         win_of, prod_of, sum_of, parked_of = {}, {}, {}, {}
 
-        def load_chunk(ch):
-            pair, u0 = ch // CHUNKS_PER_PAIR, CHUNK * (ch % CHUNKS_PER_PAIR)
-            x_rows = x_pool.tile([P, CHUNK, C], BF16)
+        def load_w(row):
+            pair, u0 = row // H, row % H
             w_rows = w_pool.tile([P, CHUNK, GROUPS * TAPS], BF16)
-            for b2 in range(2):
-                nc.sync.dma_start(
-                    out=x_rows[b2:P:2, :, :],
-                    in_=x[2 * pair + b2, u0 : u0 + CHUNK].rearrange("u v k -> v u k"),
-                )
             for b2 in range(2):
                 nc.sync.dma_start(
                     out=w_rows[b2:P:2, :, :],
                     in_=w_span[2 * pair + b2, u0 : u0 + CHUNK].rearrange("u v r -> v u r"),
                 )
-            x_of[ch], w_of[ch] = x_rows, w_rows
+            for i in range(CHUNK):
+                w_of[row + i] = w_rows[:, i, :]
 
         def sort_row(ch, k):
             x_sorted = sort_pool.tile([P, 2, P], F32)
-            nc.scalar.copy(
-                out=x_sorted[:],
-                in_=x_of[ch][:, k, :].bitcast(F32).rearrange("p (w h) -> p h w", h=2),
-            )
+            words = x_of[ch][:, k, :].bitcast(F32).rearrange("p (w h) -> p h w", h=2)
+            if ch < VECTOR_SORTS:
+                nc.vector.tensor_copy(out=x_sorted[:], in_=words)
+            else:
+                nc.scalar.copy(out=x_sorted[:], in_=words)
             sorted_of[(ch, k)] = x_sorted
 
         def turn_row(ch, k):
             if k == 0:
-                grouped = q_pool.tile([P, CHUNK * P, 4], BF16, align_bytes=64)
+                grouped = grouped_pool.tile([P, CHUNK * P, 4], BF16, align_bytes=64)
                 grouped_of[ch] = grouped
             s = k % 2
             if s == 0:
-                turned = ps_x.tile([P, 2, 2, P], F32)
-                turned_of[ch] = turned
+                if CHUNK_ROWS[ch][0] + k < EARLY_ROWS:
+                    turned = ps_win.tile([P, BANK], F32, tag="win")
+                else:
+                    turned = ps_x.tile([P, BANK], F32, tag="turned")
+                turned_of[ch] = turned[:].rearrange("p (s h n) -> p s h n", s=2, h=2)
             for half in range(2):
                 nc.tensor.transpose(turned_of[ch][:, s, half, :], sorted_of[(ch, k)][:, half, :], ident[:])
             if s == 1:
@@ -134,63 +162,77 @@ def tile_involution2d_pa_t_kernel(tc, x, Wi_words, Wi_scales, bi, w_span, out):
                     out=grouped_of[ch][:]
                     .bitcast(F32)[:, (k - 1) * P : (k + 1) * P, :]
                     .rearrange("p (s n) h -> p s n h", s=2),
-                    in_=turned_of[ch][:].rearrange("p s h n -> p s n h"),
+                    in_=turned_of[ch].rearrange("p s h n -> p s n h"),
                 )
 
         def quantise_chunk(ch):
+            pixels = CHUNK_ROWS[ch][1] * P
             codes = q_pool.tile([P, CHUNK * P], U32, align_bytes=64)
             plane = q_pool.tile([P, CHUNK * P], U8, align_bytes=64)
             nc.vector.quantize_mx(
-                out=codes[:].bitcast(FP8X4),
-                scales=plane[:],
-                in_=grouped_of[ch][:].rearrange("p n t -> p (n t)"),
+                out=codes[:, 0:pixels].bitcast(FP8X4),
+                scales=plane[:, 0:pixels],
+                in_=grouped_of[ch][:, 0:pixels, :].rearrange("p n t -> p (n t)"),
             )
             codes_of[ch], plane_of[ch] = codes, plane
 
         def project_chunk(ch):
-            pair, u0 = ch // CHUNKS_PER_PAIR, CHUNK * (ch % CHUNKS_PER_PAIR)
+            row, count = CHUNK_ROWS[ch]
+            pair, u0 = row // H, row % H
             xi_ps = ps_turns.tile([P, BANK], F32, tag="by_turns")
             nc.tensor.matmul_mx(
-                out=xi_ps[:],
+                out=xi_ps[:, 0 : count * P],
                 lhsT=wi_codes[:].bitcast(FP4X4),
                 lhsT_scale=wi_plane[:],
-                rhs=codes_of[ch][:].bitcast(FP8X4),
-                rhs_scale=plane_of[ch][:],
+                rhs=codes_of[ch][:, 0 : count * P].bitcast(FP8X4),
+                rhs_scale=plane_of[ch][:, 0 : count * P],
                 start=True,
                 stop=True,
             )
             nc.scalar.activation(
-                out=xi_img[pair][:, 1 + u0 : 1 + u0 + CHUNK, PAD : PAD + P],
-                in_=xi_ps[:].rearrange("c (u n) -> c u n", u=CHUNK),
+                out=xi_img[pair][:, 1 + u0 : 1 + u0 + count, PAD : PAD + P],
+                in_=xi_ps[:, 0 : count * P].rearrange("c (u n) -> c u n", u=count),
                 func=identity_fn,
                 bias=bias_col[:, 0:1],
                 scale=1.0,
             )
 
         def cut_windows(pair, r):
-            win = ps_win.tile([P, BANK], F32)
-            for j in range(3):
+            win = ps_win.tile([P, BANK], F32, tag="win")
+            win_of[(pair, r)] = win
+            for j in range(3) if r >= 0 else [2]:
                 start = PAD - 2 + 2 * j
                 nc.tensor.transpose(
                     win[:, P * j : P * (j + 1)], xi_img[pair][:, r + 1, start : start + P], ident[:]
                 )
-            if r < H:
-                nc.tensor.transpose(
-                    win[:, 3 * P : 4 * P], xi_img[pair][:, r + 2, PAD - 2 : PAD - 2 + P], ident[:]
-                )
-            win_of[(pair, r)] = win
+            nc.tensor.transpose(
+                win[:, 3 * P : 4 * P], xi_img[pair][:, r + 2, PAD - 2 : PAD - 2 + P], ident[:]
+            )
+
+        def open_products(pair, u):
+            prod = prod_pool.tile([P, TAPS, F], F32)
+            prod_of[(pair, u)] = prod
+            for edge, i in ((0, 0), (H - 1, 2)):
+                if u == edge:
+                    cols = slice(0, PER_GROUP * (first_group(1) - 1)) if i == 0 else slice(PER_GROUP * first_group(2), F)
+                    width = cols.stop - cols.start
+                    nc.scalar.copy(
+                        out=prod[:, :, cols],
+                        in_=xi_img[pair][:, 0, 0:width].unsqueeze(1).to_broadcast([P, TAPS, width]),
+                    )
 
         def multiply_windows(pair, r):
             win = win_of[(pair, r)]
             for i in range(3):
                 u = r + 1 - i
                 if 0 <= u < H:
-                    if i == 0:
-                        prod = prod_pool.tile([P, TAPS, F], F32)
-                        prod_of[(pair, u)] = prod
                     g0, g1 = first_group(i), first_group(i + 1)
+                    if r < 0:
+                        g0 = g1 - 1
+                    if i == 0:
+                        open_products(pair, u)
                     col = GROUP_COLS * g0 - 3 * P * i
-                    weights = w_of[pair * CHUNKS_PER_PAIR + u // CHUNK][:, u % CHUNK, TAPS * g0 : TAPS * g1]
+                    weights = w_of[H * pair + u][:, TAPS * g0 : TAPS * g1]
                     nc.vector.tensor_tensor(
                         out=prod_of[(pair, u)][:, :, PER_GROUP * g0 : PER_GROUP * g1].rearrange(
                             "p m (g e) -> p m g e", e=PER_GROUP
@@ -238,28 +280,39 @@ def tile_involution2d_pa_t_kernel(tc, x, Wi_words, Wi_scales, bi, w_span, out):
 
         plan = {}
 
-        def at(step, order, job, *args):
-            plan.setdefault(step // STRIDE, []).append((order, job, args))
+        def at_beat(beat, order, job, *args):
+            plan.setdefault(beat, []).append((order, job, args))
+
+        def at(row, beats, order, job, *args):
+            at_beat(row // BEAT + beats, order, job, *args)
+
+        def turn_beat(row):
+            p = row // 2
+            return max(p - LEAD, (p - 2 * RATE) // RATE)
 
         for pair in range(PAIRS):
-            first = STEPS_PER_PAIR * pair
-            for r in range(-1, H + 1):
-                at(first + r + 1, 2, cut_windows, pair, r)
-                at(first + r + 1, 3, multiply_windows, pair, r)
+            for r in range(-1, H):
+                row = H * pair + max(r, 0)
+                at(row, 0, 2, cut_windows, pair, r)
+                at(row, 0, 3, multiply_windows, pair, r)
             for u in range(H):
-                at(first + u + 2 + ADD_LAG, 4, add_taps, pair, u)
+                at(H * pair + u, TAP_BEATS, 4, add_taps, pair, u)
             for u0 in range(0, H, CHUNK):
-                parked = first + u0 + CHUNK + 1 + ADD_LAG
-                at(parked + 1, 5, turn_back, pair, u0)
-                ch = pair * CHUNKS_PER_PAIR + u0 // CHUNK
-                projected = first + u0 - CHUNK
-                at(projected - LOAD_LEAD, 0, load_chunk, ch)
-                for k in range(CHUNK):
-                    at(projected - SORT_LEAD + k, 1, sort_row, ch, k)
-                    at(projected - TURN_LEAD + k, 6, turn_row, ch, k)
-                at(projected - QUANT_LEAD, 7, quantise_chunk, ch)
-                at(projected, 8, project_chunk, ch)
+                at(H * pair + u0 + CHUNK, TAP_BEATS, 5, turn_back, pair, u0)
+        for ch, (row, count) in enumerate(CHUNK_ROWS):
+            turned = turn_beat(row + count - 1)
+            if ch >= len(FIRST_CHUNKS):
+                at_beat(turn_beat(row) - 6, 0, load_x, ch)
+            for k in range(count):
+                at_beat(turn_beat(row + k) - SORT_AHEAD, 1, sort_row, ch, k)
+                at_beat(turn_beat(row + k), 2.5 if row >= 4 and k < 2 and turn_beat(row) == turn_beat(row + count - 1) else 6, turn_row, ch, k)
+            at_beat(max(row // 2 - QUANT_LEAD, turned), 7, quantise_chunk, ch)
+            at_beat(max(row // 2 - PROJECT_LEAD, turned + 1), 8, project_chunk, ch)
+        at_beat(turn_beat(0) - 1, 1.5, widen_bias)
+        at_beat(turn_beat(0), 6.5, turn_bias)
+        for row in range(0, ROWS, CHUNK):
+            at(row, -4, 0.5, load_w, row)
 
-        for step in sorted(plan):
-            for order, job, args in sorted(plan[step], key=lambda entry: entry[0]):
+        for beat in sorted(plan):
+            for order, job, args in sorted(plan[beat], key=lambda entry: entry[0]):
                 job(*args)

@@ -39,6 +39,9 @@ SORT_AHEAD = 1
 QUANT_LEAD = 5
 PROJECT_LEAD = 3
 
+FOLDED = 1
+SUMMED = TAPS - FOLDED
+
 FLOPS = 2 * IMAGES * H * W * C * F + 2 * IMAGES * H * W * TAPS * F
 
 
@@ -55,7 +58,7 @@ def tile_involution2d_pa_t_kernel(tc, x, Wi_words, Wi_scales, bi, w_span, out):
         const = ctx.enter_context(tc.tile_pool(name="const", bufs=1))
         x_pool = ctx.enter_context(tc.tile_pool(name="x_pool", bufs=6))
         w_pool = ctx.enter_context(tc.tile_pool(name="w_pool", bufs=5))
-        sort_pool = ctx.enter_context(tc.tile_pool(name="sort_pool", bufs=12))
+        sort_pool = ctx.enter_context(tc.tile_pool(name="sort_pool", bufs=6))
         grouped_pool = ctx.enter_context(tc.tile_pool(name="grouped_pool", bufs=7))
         q_pool = ctx.enter_context(tc.tile_pool(name="q_pool", bufs=3))
         prod_pool = ctx.enter_context(tc.tile_pool(name="prod_pool", bufs=2 * TAP_BEATS + 4))
@@ -135,14 +138,16 @@ def tile_involution2d_pa_t_kernel(tc, x, Wi_words, Wi_scales, bi, w_span, out):
             for i in range(CHUNK):
                 w_of[row + i] = w_rows[:, i, :]
 
-        def sort_row(ch, k):
-            x_sorted = sort_pool.tile([P, 2, P], F32)
-            words = x_of[ch][:, k, :].bitcast(F32).rearrange("p (w h) -> p h w", h=2)
+        def sort_rows(ch, k):
+            x_sorted = sort_pool.tile([P, 2, 2, P], F32)
+            words = x_of[ch][:, k : k + 2, :].bitcast(F32).rearrange("p s (w h) -> p s w h", h=2)
+            into = x_sorted[:].rearrange("p s h w -> p s w h")
             if ch < VECTOR_SORTS:
-                nc.vector.tensor_copy(out=x_sorted[:], in_=words)
+                nc.vector.tensor_copy(out=into, in_=words)
             else:
-                nc.scalar.copy(out=x_sorted[:], in_=words)
-            sorted_of[(ch, k)] = x_sorted
+                nc.scalar.copy(out=into, in_=words)
+            sorted_of[(ch, k)] = x_sorted[:, 0]
+            sorted_of[(ch, k + 1)] = x_sorted[:, 1]
 
         def turn_row(ch, k):
             if k == 0:
@@ -156,7 +161,7 @@ def tile_involution2d_pa_t_kernel(tc, x, Wi_words, Wi_scales, bi, w_span, out):
                     turned = ps_x.tile([P, BANK], F32, tag="turned")
                 turned_of[ch] = turned[:].rearrange("p (s h n) -> p s h n", s=2, h=2)
             for half in range(2):
-                nc.tensor.transpose(turned_of[ch][:, s, half, :], sorted_of[(ch, k)][:, half, :], ident[:])
+                nc.tensor.transpose(turned_of[ch][:, s, half, :], sorted_of[(ch, k)][:, half], ident[:])
             if s == 1:
                 nc.scalar.copy(
                     out=grouped_of[ch][:]
@@ -246,19 +251,28 @@ def tile_involution2d_pa_t_kernel(tc, x, Wi_words, Wi_scales, bi, w_span, out):
                         op=mult,
                     )
 
+        def fold_taps(pair, u):
+            prod = prod_of[(pair, u)]
+            nc.gpsimd.tensor_tensor(
+                out=prod[:, SUMMED - FOLDED : SUMMED, :],
+                in0=prod[:, SUMMED - FOLDED : SUMMED, :],
+                in1=prod[:, SUMMED:TAPS, :],
+                op=mybir.AluOpType.add,
+            )
+
         def add_taps(pair, u):
             slot = u % CHUNK
             if slot == 0:
                 sum_ps = ps_sum.tile([P, BANK], F32)
                 sum_of[pair] = sum_ps
-            for m in range(TAPS):
+            for m in range(SUMMED):
                 nc.tensor.matmul(
                     out=sum_of[pair][:, P * slot : P * (slot + 1)],
                     lhsT=prod_of[(pair, u)][:, m, :],
                     rhs=ident[:],
                     is_transpose=True,
                     start=(m == 0),
-                    stop=(m == TAPS - 1),
+                    stop=(m == SUMMED - 1),
                 )
             if slot == CHUNK - 1:
                 sum_sb = out_pool.tile([P, BANK], F32)
@@ -273,7 +287,7 @@ def tile_involution2d_pa_t_kernel(tc, x, Wi_words, Wi_scales, bi, w_span, out):
             out_rows = out_pool.tile([P, CHUNK, F], F32)
             nc.scalar.copy(out=out_rows[:], in_=back_ps[:].rearrange("p (u o) -> p u o", u=CHUNK))
             for b2 in range(2):
-                nc.scalar.dma_start(
+                nc.sync.dma_start(
                     out=out[2 * pair + b2, u0 : u0 + CHUNK].rearrange("u v o -> v u o"),
                     in_=out_rows[b2:P:2, :, :],
                 )
@@ -295,6 +309,9 @@ def tile_involution2d_pa_t_kernel(tc, x, Wi_words, Wi_scales, bi, w_span, out):
                 row = H * pair + max(r, 0)
                 at(row, 0, 2, cut_windows, pair, r)
                 at(row, 0, 3, multiply_windows, pair, r)
+                for u in [r - 1] if r < H - 1 else [r - 1, r]:
+                    if u >= 0:
+                        at(row, 0, 3.5, fold_taps, pair, u)
             for u in range(H):
                 at(H * pair + u, TAP_BEATS, 4, add_taps, pair, u)
             for u0 in range(0, H, CHUNK):
@@ -304,7 +321,8 @@ def tile_involution2d_pa_t_kernel(tc, x, Wi_words, Wi_scales, bi, w_span, out):
             if ch >= len(FIRST_CHUNKS):
                 at_beat(turn_beat(row) - 6, 0, load_x, ch)
             for k in range(count):
-                at_beat(turn_beat(row + k) - SORT_AHEAD, 1, sort_row, ch, k)
+                if k % 2 == 0:
+                    at_beat(turn_beat(row + k) - SORT_AHEAD, 1, sort_rows, ch, k)
                 at_beat(turn_beat(row + k), 2.5 if row >= 4 and k < 2 and turn_beat(row) == turn_beat(row + count - 1) else 6, turn_row, ch, k)
             at_beat(max(row // 2 - QUANT_LEAD, turned), 7, quantise_chunk, ch)
             at_beat(max(row // 2 - PROJECT_LEAD, turned + 1), 8, project_chunk, ch)

@@ -240,14 +240,14 @@ def tile_involution2d_pa_t_kernel(tc, x, Wi_words, Wi_scales, bi, w_span, out):
                     weights = w_of[H * pair + u][:, TAPS * g0 : TAPS * g1]
                     nc.vector.tensor_tensor(
                         out=prod_of[(pair, u)][:, :, PER_GROUP * g0 : PER_GROUP * g1].rearrange(
-                            "p m (g e) -> p m g e", e=PER_GROUP
+                            "p m (g e) -> p g m e", e=PER_GROUP
                         ),
                         in0=win[:, col : col + GROUP_COLS * (g1 - g0)].rearrange(
-                            "p (g e m) -> p m g e", e=PER_GROUP, m=TAPS
+                            "p (g e m) -> p g m e", e=PER_GROUP, m=TAPS
                         ),
-                        in1=weights.rearrange("p (g m) -> p m g", m=TAPS)
+                        in1=weights.rearrange("p (g m) -> p g m", m=TAPS)
                         .unsqueeze(3)
-                        .to_broadcast([P, TAPS, g1 - g0, PER_GROUP]),
+                        .to_broadcast([P, g1 - g0, TAPS, PER_GROUP]),
                         op=mult,
                     )
 

@@ -33,13 +33,16 @@ CHUNK_ROWS = FIRST_CHUNKS + [(row, CHUNK) for row in range(4, ROWS, CHUNK)]
 
 LEAD = 6
 RATE = 2
+RATE_D = 1
+Q2 = 3
 EARLY_ROWS = 12
 VECTOR_SORTS = 4
 SORT_AHEAD = 1
 QUANT_LEAD = 5
 PROJECT_LEAD = 3
 
-FOLDED = 1
+LAST_STORE = 2
+FOLDED = 2
 SUMMED = TAPS - FOLDED
 
 FLOPS = 2 * IMAGES * H * W * C * F + 2 * IMAGES * H * W * TAPS * F
@@ -68,6 +71,10 @@ def tile_involution2d_pa_t_kernel(tc, x, Wi_words, Wi_scales, bi, w_span, out):
         ps_sum = ctx.enter_context(tc.psum_pool(name="ps_sum", bufs=2))
         ps_turns = ctx.enter_context(tc.psum_pool(name="ps_turns", bufs=1))
         ctx.enter_context(tc.manual_schedule())
+
+        bias_bf = const.tile([P, F], BF16)
+        nc.vector.memset(bias_bf[:], 0.0)
+        nc.scalar.dma_start(out=bias_bf[0:1, :], in_=bi.rearrange("(o f) -> o f", o=1))
 
         warm = const.tile([P, 1], F32)
         nc.vector.memset(warm[:], 0.0)
@@ -102,9 +109,6 @@ def tile_involution2d_pa_t_kernel(tc, x, Wi_words, Wi_scales, bi, w_span, out):
                 in_=Wi_scales[0, 4 * quadrant : 4 * quadrant + 4, :].bitcast(I32),
             )
 
-        bias_bf = const.tile([P, F], BF16)
-        nc.vector.memset(bias_bf[:], 0.0)
-        nc.scalar.dma_start(out=bias_bf[0:1, :], in_=bi.rearrange("(o f) -> o f", o=1))
         bias_rows = const.tile([P, F], F32)
         bias_col = const.tile([P, 1], F32)
 
@@ -226,30 +230,37 @@ def tile_involution2d_pa_t_kernel(tc, x, Wi_words, Wi_scales, bi, w_span, out):
                         in_=xi_img[pair][:, 0, 0:width].unsqueeze(1).to_broadcast([P, TAPS, width]),
                     )
 
-        def multiply_windows(pair, r):
-            win = win_of[(pair, r)]
-            for i in range(3):
-                u = r + 1 - i
-                if 0 <= u < H:
-                    g0, g1 = first_group(i), first_group(i + 1)
-                    if r < 0:
-                        g0 = g1 - 1
-                    if i == 0:
-                        open_products(pair, u)
-                    col = GROUP_COLS * g0 - 3 * P * i
-                    weights = w_of[H * pair + u][:, TAPS * g0 : TAPS * g1]
-                    nc.vector.tensor_tensor(
-                        out=prod_of[(pair, u)][:, :, PER_GROUP * g0 : PER_GROUP * g1].rearrange(
-                            "p m (g e) -> p g m e", e=PER_GROUP
-                        ),
-                        in0=win[:, col : col + GROUP_COLS * (g1 - g0)].rearrange(
-                            "p (g e m) -> p g m e", e=PER_GROUP, m=TAPS
-                        ),
-                        in1=weights.rearrange("p (g m) -> p g m", m=TAPS)
-                        .unsqueeze(3)
-                        .to_broadcast([P, g1 - g0, TAPS, PER_GROUP]),
-                        op=mult,
-                    )
+        def multiply_windows(pair, r, i):
+            u = r + 1 - i
+            if u < 0 or u >= H:
+                return
+            g0, g1 = first_group(i), first_group(i + 1)
+            if r < 0:
+                g0 = g1 - 1
+            if i == 0:
+                open_products(pair, u)
+            col = GROUP_COLS * g0 - 3 * P * i
+            weights = w_of[H * pair + u][:, TAPS * g0 : TAPS * g1]
+            nc.vector.tensor_tensor(
+                out=prod_of[(pair, u)][:, :, PER_GROUP * g0 : PER_GROUP * g1].rearrange(
+                    "p m (g e) -> p g m e", e=PER_GROUP
+                ),
+                in0=win_of[(pair, r)][:, col : col + GROUP_COLS * (g1 - g0)].rearrange(
+                    "p (g e m) -> p g m e", e=PER_GROUP, m=TAPS
+                ),
+                in1=weights.rearrange("p (g m) -> p g m", m=TAPS)
+                .unsqueeze(3)
+                .to_broadcast([P, g1 - g0, TAPS, PER_GROUP]),
+                op=mult,
+            )
+
+        def store_group(pair, u):
+            if H * pair + u >= ROWS - CHUNK:
+                return u - u % LAST_STORE, LAST_STORE
+            return u - u % CHUNK, CHUNK
+
+        def folded(pair, u):
+            return H * pair + u < ROWS - LAST_STORE
 
         def fold_taps(pair, u):
             prod = prod_of[(pair, u)]
@@ -261,35 +272,40 @@ def tile_involution2d_pa_t_kernel(tc, x, Wi_words, Wi_scales, bi, w_span, out):
             )
 
         def add_taps(pair, u):
-            slot = u % CHUNK
+            u0, count = store_group(pair, u)
+            slot = u - u0
             if slot == 0:
                 sum_ps = ps_sum.tile([P, BANK], F32)
                 sum_of[pair] = sum_ps
-            for m in range(SUMMED):
+            taps = SUMMED if folded(pair, u) else TAPS
+            for m in range(taps):
                 nc.tensor.matmul(
                     out=sum_of[pair][:, P * slot : P * (slot + 1)],
                     lhsT=prod_of[(pair, u)][:, m, :],
                     rhs=ident[:],
                     is_transpose=True,
                     start=(m == 0),
-                    stop=(m == SUMMED - 1),
+                    stop=(m == taps - 1),
                 )
-            if slot == CHUNK - 1:
+            if slot == count - 1:
                 sum_sb = out_pool.tile([P, BANK], F32)
-                nc.scalar.copy(out=sum_sb[:], in_=sum_of[pair][:])
-                parked_of[(pair, u - slot)] = sum_sb
+                nc.scalar.copy(out=sum_sb[:, 0 : P * count], in_=sum_of[pair][:, 0 : P * count])
+                parked_of[(pair, u0)] = sum_sb
 
         def turn_back(pair, u0):
             back_ps = ps_turns.tile([P, BANK], F32, tag="by_turns")
-            for slot in range(CHUNK):
+            count = store_group(pair, u0)[1]
+            for slot in range(count):
                 cols = slice(P * slot, P * (slot + 1))
                 nc.tensor.transpose(back_ps[:, cols], parked_of[(pair, u0)][:, cols], ident[:])
             out_rows = out_pool.tile([P, CHUNK, F], F32)
-            nc.scalar.copy(out=out_rows[:], in_=back_ps[:].rearrange("p (u o) -> p u o", u=CHUNK))
+            nc.scalar.copy(
+                out=out_rows[:, 0:count, :], in_=back_ps[:, 0 : P * count].rearrange("p (u o) -> p u o", u=count)
+            )
             for b2 in range(2):
                 nc.sync.dma_start(
-                    out=out[2 * pair + b2, u0 : u0 + CHUNK].rearrange("u v o -> v u o"),
-                    in_=out_rows[b2:P:2, :, :],
+                    out=out[2 * pair + b2, u0 : u0 + count].rearrange("u v o -> v u o"),
+                    in_=out_rows[b2:P:2, 0:count, :],
                 )
 
         plan = {}
@@ -302,34 +318,40 @@ def tile_involution2d_pa_t_kernel(tc, x, Wi_words, Wi_scales, bi, w_span, out):
 
         def turn_beat(row):
             p = row // 2
-            return max(p - LEAD, (p - 2 * RATE) // RATE)
+            return max(p - LEAD, (p - 4) * RATE_D // RATE)
 
         for pair in range(PAIRS):
             for r in range(-1, H):
                 row = H * pair + max(r, 0)
                 at(row, 0, 2, cut_windows, pair, r)
-                at(row, 0, 3, multiply_windows, pair, r)
+                for i in range(3):
+                    at(row, 0, 3, multiply_windows, pair, r, i)
                 for u in [r - 1] if r < H - 1 else [r - 1, r]:
-                    if u >= 0:
+                    if u >= 0 and folded(pair, u):
                         at(row, 0, 3.5, fold_taps, pair, u)
             for u in range(H):
                 at(H * pair + u, TAP_BEATS, 4, add_taps, pair, u)
-            for u0 in range(0, H, CHUNK):
-                at(H * pair + u0 + CHUNK, TAP_BEATS, 5, turn_back, pair, u0)
+                u0, count = store_group(pair, u)
+                if u == u0:
+                    at(H * pair + u0 + count, TAP_BEATS, 5, turn_back, pair, u0)
         for ch, (row, count) in enumerate(CHUNK_ROWS):
             turned = turn_beat(row + count - 1)
             if ch >= len(FIRST_CHUNKS):
                 at_beat(turn_beat(row) - 6, 0, load_x, ch)
             for k in range(count):
                 if k % 2 == 0:
-                    at_beat(turn_beat(row + k) - SORT_AHEAD, 1, sort_rows, ch, k)
+                    beat = turn_beat(row + k) - SORT_AHEAD
+                    at_beat(beat, 1 if beat < turn_beat(0) or beat >= 0 else 7.5, sort_rows, ch, k)
                 at_beat(turn_beat(row + k), 2.5 if row >= 4 and k < 2 and turn_beat(row) == turn_beat(row + count - 1) else 6, turn_row, ch, k)
-            at_beat(max(row // 2 - QUANT_LEAD, turned), 7, quantise_chunk, ch)
-            at_beat(max(row // 2 - PROJECT_LEAD, turned + 1), 8, project_chunk, ch)
-        at_beat(turn_beat(0) - 1, 1.5, widen_bias)
+            if ch == len(FIRST_CHUNKS):
+                at_beat(0, Q2, quantise_chunk, ch)
+            else:
+                at_beat(max(row // 2 - QUANT_LEAD, turned), 7, quantise_chunk, ch)
+            at_beat(max(row // 2 - PROJECT_LEAD, turned + (ch >= len(FIRST_CHUNKS))), 8, project_chunk, ch)
+        at_beat(turn_beat(0), 6.5, widen_bias)
         at_beat(turn_beat(0), 6.5, turn_bias)
         for row in range(0, ROWS, CHUNK):
-            at(row, -4, 0.5, load_w, row)
+            at_beat(row // BEAT - 4 if row else turn_beat(0) - 9, 0.5, load_w, row)
 
         for beat in sorted(plan):
             for order, job, args in sorted(plan[beat], key=lambda entry: entry[0]):

from contextlib import ExitStack

import concourse.mybir as mybir
from concourse.masks import make_identity

F32 = mybir.dt.float32
BF16 = mybir.dt.bfloat16
I32 = mybir.dt.int32
U32 = mybir.dt.uint32
U8 = mybir.dt.uint8
FP8X4 = mybir.dt.float8_e4m3fn_x4
FP4X4 = mybir.dt.float4_e2m1fn_x4

P = 128
IMAGES, H, W, C, F = 4, 64, 64, 512, 128
PAIRS = IMAGES // 2
TAPS = 9
GROUPS = 16
PER_GROUP = F // GROUPS
GROUP_COLS = PER_GROUP * TAPS
CHUNK = 4
ROWS = PAIRS * H
BANK = 512
PAD = 8
ROW_COLS = PAD + P + PAD

WIN_BANKS = 4
TAP_BEATS = 2
BEAT = 2

FIRST_CHUNKS = [(0, 2), (2, 2)]
CHUNK_ROWS = FIRST_CHUNKS + [(row, CHUNK) for row in range(4, ROWS, CHUNK)]

LEAD = 6
RATE = 2
RATE_D = 1
Q2 = 3
EARLY_ROWS = 12
VECTOR_SORTS = 4
SORT_AHEAD = 1
QUANT_LEAD = 5
PROJECT_LEAD = 3

LAST_STORE = 2
FOLDED = 2
SUMMED = TAPS - FOLDED

FLOPS = 2 * IMAGES * H * W * C * F + 2 * IMAGES * H * W * TAPS * F


def first_group(i):
    return -(-3 * P * i // GROUP_COLS)


def tile_involution2d_pa_t_kernel(tc, x, Wi_words, Wi_scales, bi, w_span, out):
    nc = tc.nc
    mult = mybir.AluOpType.mult
    identity_fn = mybir.ActivationFunctionType.Identity

    with ExitStack() as ctx:
        const = ctx.enter_context(tc.tile_pool(name="const", bufs=1))
        x_pool = ctx.enter_context(tc.tile_pool(name="x_pool", bufs=6))
        w_pool = ctx.enter_context(tc.tile_pool(name="w_pool", bufs=5))
        sort_pool = ctx.enter_context(tc.tile_pool(name="sort_pool", bufs=6))
        grouped_pool = ctx.enter_context(tc.tile_pool(name="grouped_pool", bufs=7))
        q_pool = ctx.enter_context(tc.tile_pool(name="q_pool", bufs=3))
        prod_pool = ctx.enter_context(tc.tile_pool(name="prod_pool", bufs=2 * TAP_BEATS + 4))
        out_pool = ctx.enter_context(tc.tile_pool(name="out_pool", bufs=3))
        ps_x = ctx.enter_context(tc.psum_pool(name="ps_x", bufs=1))
        ps_win = ctx.enter_context(tc.psum_pool(name="ps_win", bufs=WIN_BANKS))
        ps_sum = ctx.enter_context(tc.psum_pool(name="ps_sum", bufs=2))
        ps_turns = ctx.enter_context(tc.psum_pool(name="ps_turns", bufs=1))
        ctx.enter_context(tc.manual_schedule())

        bias_bf = const.tile([P, F], BF16)
        nc.vector.memset(bias_bf[:], 0.0)
        nc.scalar.dma_start(out=bias_bf[0:1, :], in_=bi.rearrange("(o f) -> o f", o=1))

        warm = const.tile([P, 1], F32)
        nc.vector.memset(warm[:], 0.0)
        nc.scalar.activation(out=warm[:], in_=warm[:], func=identity_fn, bias=0.0, scale=1.0)

        x_of, w_of, sorted_of, turned_of, grouped_of, codes_of, plane_of = {}, {}, {}, {}, {}, {}, {}

        def load_x(ch):
            row, count = CHUNK_ROWS[ch]
            pair, u0 = row // H, row % H
            x_rows = x_pool.tile([P, CHUNK, C], BF16)
            for b2 in range(2):
                nc.sync.dma_start(
                    out=x_rows[b2:P:2, 0:count, :],
                    in_=x[2 * pair + b2, u0 : u0 + count].rearrange("u v k -> v u k"),
                )
            x_of[ch] = x_rows

        for ch in range(len(FIRST_CHUNKS)):
            load_x(ch)

        ident = const.tile([P, P], F32)
        make_identity(nc, ident[:])

        wi_codes = const.tile([P, 2 * F], U8, align_bytes=64)
        wi_plane = const.tile([P, F], U8, align_bytes=64)
        nc.vector.memset(wi_plane[:].bitcast(I32), 0)
        nc.sync.dma_start(out=wi_codes[:].bitcast(I32), in_=Wi_words[0].bitcast(I32))
        for quadrant in range(4):
            nc.sync.dma_start(
                out=wi_plane[32 * quadrant : 32 * quadrant + 4, :].bitcast(I32),
                in_=Wi_scales[0, 4 * quadrant : 4 * quadrant + 4, :].bitcast(I32),
            )

        bias_rows = const.tile([P, F], F32)
        bias_col = const.tile([P, 1], F32)

        def widen_bias():
            nc.vector.tensor_copy(out=bias_rows[:], in_=bias_bf[:])

        def turn_bias():
            bias_ps = ps_turns.tile([P, BANK], F32, tag="by_turns")
            nc.tensor.transpose(bias_ps[:, 0:P], bias_rows[:], ident[:])
            nc.vector.tensor_copy(out=bias_col[:], in_=bias_ps[:, 0:1])

        xi_img = []
        for pair in range(PAIRS):
            xi_pair = const.tile([P, H + 2, ROW_COLS], F32, name="xi_pair%d" % pair)
            nc.gpsimd.memset(xi_pair[:, :, 0:PAD], 0.0)
            nc.gpsimd.memset(xi_pair[:, :, PAD + P : ROW_COLS], 0.0)
            nc.gpsimd.memset(xi_pair[:, 0, PAD : PAD + P], 0.0)
            nc.gpsimd.memset(xi_pair[:, H + 1, PAD : PAD + P], 0.0)
            xi_img.append(xi_pair)

        win_of, prod_of, sum_of, parked_of = {}, {}, {}, {}

        def load_w(row):
            pair, u0 = row // H, row % H
            w_rows = w_pool.tile([P, CHUNK, GROUPS * TAPS], BF16)
            for b2 in range(2):
                nc.sync.dma_start(
                    out=w_rows[b2:P:2, :, :],
                    in_=w_span[2 * pair + b2, u0 : u0 + CHUNK].rearrange("u v r -> v u r"),
                )
            for i in range(CHUNK):
                w_of[row + i] = w_rows[:, i, :]

        def sort_rows(ch, k):
            x_sorted = sort_pool.tile([P, 2, 2, P], F32)
            words = x_of[ch][:, k : k + 2, :].bitcast(F32).rearrange("p s (w h) -> p s w h", h=2)
            into = x_sorted[:].rearrange("p s h w -> p s w h")
            if ch < VECTOR_SORTS:
                nc.vector.tensor_copy(out=into, in_=words)
            else:
                nc.scalar.copy(out=into, in_=words)
            sorted_of[(ch, k)] = x_sorted[:, 0]
            sorted_of[(ch, k + 1)] = x_sorted[:, 1]

        def turn_row(ch, k):
            if k == 0:
                grouped = grouped_pool.tile([P, CHUNK * P, 4], BF16, align_bytes=64)
                grouped_of[ch] = grouped
            s = k % 2
            if s == 0:
                if CHUNK_ROWS[ch][0] + k < EARLY_ROWS:
                    turned = ps_win.tile([P, BANK], F32, tag="win")
                else:
                    turned = ps_x.tile([P, BANK], F32, tag="turned")
                turned_of[ch] = turned[:].rearrange("p (s h n) -> p s h n", s=2, h=2)
            for half in range(2):
                nc.tensor.transpose(turned_of[ch][:, s, half, :], sorted_of[(ch, k)][:, half], ident[:])
            if s == 1:
                nc.scalar.copy(
                    out=grouped_of[ch][:]
                    .bitcast(F32)[:, (k - 1) * P : (k + 1) * P, :]
                    .rearrange("p (s n) h -> p s n h", s=2),
                    in_=turned_of[ch].rearrange("p s h n -> p s n h"),
                )

        def quantise_chunk(ch):
            pixels = CHUNK_ROWS[ch][1] * P
            codes = q_pool.tile([P, CHUNK * P], U32, align_bytes=64)
            plane = q_pool.tile([P, CHUNK * P], U8, align_bytes=64)
            nc.vector.quantize_mx(
                out=codes[:, 0:pixels].bitcast(FP8X4),
                scales=plane[:, 0:pixels],
                in_=grouped_of[ch][:, 0:pixels, :].rearrange("p n t -> p (n t)"),
            )
            codes_of[ch], plane_of[ch] = codes, plane

        def project_chunk(ch):
            row, count = CHUNK_ROWS[ch]
            pair, u0 = row // H, row % H
            xi_ps = ps_turns.tile([P, BANK], F32, tag="by_turns")
            nc.tensor.matmul_mx(
                out=xi_ps[:, 0 : count * P],
                lhsT=wi_codes[:].bitcast(FP4X4),
                lhsT_scale=wi_plane[:],
                rhs=codes_of[ch][:, 0 : count * P].bitcast(FP8X4),
                rhs_scale=plane_of[ch][:, 0 : count * P],
                start=True,
                stop=True,
            )
            nc.scalar.activation(
                out=xi_img[pair][:, 1 + u0 : 1 + u0 + count, PAD : PAD + P],
                in_=xi_ps[:, 0 : count * P].rearrange("c (u n) -> c u n", u=count),
                func=identity_fn,
                bias=bias_col[:, 0:1],
                scale=1.0,
            )

        def cut_windows(pair, r):
            win = ps_win.tile([P, BANK], F32, tag="win")
            win_of[(pair, r)] = win
            for j in range(3) if r >= 0 else [2]:
                start = PAD - 2 + 2 * j
                nc.tensor.transpose(
                    win[:, P * j : P * (j + 1)], xi_img[pair][:, r + 1, start : start + P], ident[:]
                )
            nc.tensor.transpose(
                win[:, 3 * P : 4 * P], xi_img[pair][:, r + 2, PAD - 2 : PAD - 2 + P], ident[:]
            )

        def open_products(pair, u):
            prod = prod_pool.tile([P, TAPS, F], F32)
            prod_of[(pair, u)] = prod
            for edge, i in ((0, 0), (H - 1, 2)):
                if u == edge:
                    cols = slice(0, PER_GROUP * (first_group(1) - 1)) if i == 0 else slice(PER_GROUP * first_group(2), F)
                    width = cols.stop - cols.start
                    nc.scalar.copy(
                        out=prod[:, :, cols],
                        in_=xi_img[pair][:, 0, 0:width].unsqueeze(1).to_broadcast([P, TAPS, width]),
                    )

        def multiply_windows(pair, r, i):
            u = r + 1 - i
            if u < 0 or u >= H:
                return
            g0, g1 = first_group(i), first_group(i + 1)
            if r < 0:
                g0 = g1 - 1
            if i == 0:
                open_products(pair, u)
            col = GROUP_COLS * g0 - 3 * P * i
            weights = w_of[H * pair + u][:, TAPS * g0 : TAPS * g1]
            nc.vector.tensor_tensor(
                out=prod_of[(pair, u)][:, :, PER_GROUP * g0 : PER_GROUP * g1].rearrange(
                    "p m (g e) -> p g m e", e=PER_GROUP
                ),
                in0=win_of[(pair, r)][:, col : col + GROUP_COLS * (g1 - g0)].rearrange(
                    "p (g e m) -> p g m e", e=PER_GROUP, m=TAPS
                ),
                in1=weights.rearrange("p (g m) -> p g m", m=TAPS)
                .unsqueeze(3)
                .to_broadcast([P, g1 - g0, TAPS, PER_GROUP]),
                op=mult,
            )

        def store_group(pair, u):
            if H * pair + u >= ROWS - CHUNK:
                return u - u % LAST_STORE, LAST_STORE
            return u - u % CHUNK, CHUNK

        def folded(pair, u):
            return H * pair + u < ROWS - LAST_STORE

        def fold_taps(pair, u):
            prod = prod_of[(pair, u)]
            nc.gpsimd.tensor_tensor(
                out=prod[:, SUMMED - FOLDED : SUMMED, :],
                in0=prod[:, SUMMED - FOLDED : SUMMED, :],
                in1=prod[:, SUMMED:TAPS, :],
                op=mybir.AluOpType.add,
            )

        def add_taps(pair, u):
            u0, count = store_group(pair, u)
            slot = u - u0
            if slot == 0:
                sum_ps = ps_sum.tile([P, BANK], F32)
                sum_of[pair] = sum_ps
            taps = SUMMED if folded(pair, u) else TAPS
            for m in range(taps):
                nc.tensor.matmul(
                    out=sum_of[pair][:, P * slot : P * (slot + 1)],
                    lhsT=prod_of[(pair, u)][:, m, :],
                    rhs=ident[:],
                    is_transpose=True,
                    start=(m == 0),
                    stop=(m == taps - 1),
                )
            if slot == count - 1:
                sum_sb = out_pool.tile([P, BANK], F32)
                nc.scalar.copy(out=sum_sb[:, 0 : P * count], in_=sum_of[pair][:, 0 : P * count])
                parked_of[(pair, u0)] = sum_sb

        def turn_back(pair, u0):
            back_ps = ps_turns.tile([P, BANK], F32, tag="by_turns")
            count = store_group(pair, u0)[1]
            for slot in range(count):
                cols = slice(P * slot, P * (slot + 1))
                nc.tensor.transpose(back_ps[:, cols], parked_of[(pair, u0)][:, cols], ident[:])
            out_rows = out_pool.tile([P, CHUNK, F], F32)
            nc.scalar.copy(
                out=out_rows[:, 0:count, :], in_=back_ps[:, 0 : P * count].rearrange("p (u o) -> p u o", u=count)
            )
            for b2 in range(2):
                nc.sync.dma_start(
                    out=out[2 * pair + b2, u0 : u0 + count].rearrange("u v o -> v u o"),
                    in_=out_rows[b2:P:2, 0:count, :],
                )

        plan = {}

        def at_beat(beat, order, job, *args):
            plan.setdefault(beat, []).append((order, job, args))

        def at(row, beats, order, job, *args):
            at_beat(row // BEAT + beats, order, job, *args)

        def turn_beat(row):
            p = row // 2
            return max(p - LEAD, (p - 4) * RATE_D // RATE)

        for pair in range(PAIRS):
            for r in range(-1, H):
                row = H * pair + max(r, 0)
                at(row, 0, 2, cut_windows, pair, r)
                for i in range(3):
                    at(row, 0, 3, multiply_windows, pair, r, i)
                for u in [r - 1] if r < H - 1 else [r - 1, r]:
                    if u >= 0 and folded(pair, u):
                        at(row, 0, 3.5, fold_taps, pair, u)
            for u in range(H):
                at(H * pair + u, TAP_BEATS, 4, add_taps, pair, u)
                u0, count = store_group(pair, u)
                if u == u0:
                    at(H * pair + u0 + count, TAP_BEATS, 5, turn_back, pair, u0)
        for ch, (row, count) in enumerate(CHUNK_ROWS):
            turned = turn_beat(row + count - 1)
            if ch >= len(FIRST_CHUNKS):
                at_beat(turn_beat(row) - 6, 0, load_x, ch)
            for k in range(count):
                if k % 2 == 0:
                    beat = turn_beat(row + k) - SORT_AHEAD
                    at_beat(beat, 1 if beat < turn_beat(0) or beat >= 0 else 7.5, sort_rows, ch, k)
                at_beat(turn_beat(row + k), 2.5 if row >= 4 and k < 2 and turn_beat(row) == turn_beat(row + count - 1) else 6, turn_row, ch, k)
            if ch == len(FIRST_CHUNKS):
                at_beat(0, Q2, quantise_chunk, ch)
            else:
                at_beat(max(row // 2 - QUANT_LEAD, turned), 7, quantise_chunk, ch)
            at_beat(max(row // 2 - PROJECT_LEAD, turned + (ch >= len(FIRST_CHUNKS))), 8, project_chunk, ch)
        at_beat(turn_beat(0), 6.5, widen_bias)
        at_beat(turn_beat(0), 6.5, turn_bias)
        for row in range(0, ROWS, CHUNK):
            at_beat(row // BEAT - 4 if row else turn_beat(0) - 9, 0.5, load_w, row)

        for beat in sorted(plan):
            for order, job, args in sorted(plan[beat], key=lambda entry: entry[0]):
                job(*args)
